import numpy as np
import ml_dtypes


def mxq(x, axis, fmt="e4m3"):
    dtype, down = {"e4m3": (ml_dtypes.float8_e4m3fn, 7), "e5m2": (ml_dtypes.float8_e5m2, 14)}[fmt]
    v = np.moveaxis(np.asarray(x, np.float32).astype(ml_dtypes.bfloat16).astype(np.float64), axis, -1)
    blocks = v.reshape(v.shape[:-1] + (-1, 32))
    amax = np.abs(blocks).max(-1, keepdims=True)
    byte = np.maximum(np.where(amax > 0, np.frexp(amax)[1] - 1 + 127, 0) - down, 1)
    scale = np.exp2(byte - 127.0)
    codes = (blocks / scale).astype(np.float32).astype(dtype).astype(np.float64)
    return np.moveaxis((codes * scale).reshape(v.shape), -1, axis)


WIDE = False


def mx_kscale(k):
    if not WIDE:
        return np.ones(k)
    levels = np.array([10, -10, 5, -5, 0])
    if k % 512:
        return np.exp2(np.random.permutation(np.resize(levels, k // 32))).repeat(32)
    a = np.empty((k // 512, 16))
    for p in range(k // 512):
        a[p, :8] = np.random.permutation(np.resize(levels, 8))
        for g in range(8):
            far = levels[np.abs(levels - a[p, g]) >= 10]
            a[p, g + 8] = far[np.random.randint(len(far))]
    return np.exp2(a.ravel()).repeat(32)


BF16 = ml_dtypes.bfloat16


def bf(x):
    return np.asarray(x, np.float32).astype(BF16)


def f64(x):
    return np.asarray(x).astype(np.float64)


B, S, D, BD, K = 4, 1024, 1024, 512, 128
TS = 3.0


def sigmoid(v):
    return 1.0 / (1.0 + np.exp(-v))


def setup_inputs():
    s = mx_kscale(D)
    return {
        "token_embeddings": bf(np.random.standard_normal((B, S, D)) * TS * s),
        "splat_influences": bf(np.random.uniform(size=(B, S, K))),
        "decoded": bf(np.random.standard_normal((B, K, D)) * 0.35),
        "gate_W": bf(np.random.standard_normal((D, D)) / (TS * np.sqrt(D)) / s[:, None]),
        "gate_b": bf(np.random.standard_normal(D) * 0.5),
    }


def core(token_embeddings, splat_influences, decoded, gate_W, gate_b):
    flow = f64(splat_influences) @ f64(decoded)
    gate = sigmoid((mxq(f64(token_embeddings), 2, "e4m3") @ mxq(f64(gate_W), 0, "e4m3")) + f64(gate_b))
    return flow * gate


def e4m3fn_bytes(y):
    return np.clip(np.asarray(y, np.float64), -448.0, 448.0).astype(np.float32).astype(ml_dtypes.float8_e4m3fn).view(np.uint8)


Y_SCALE = 160.0


def reference(token_embeddings, splat_influences, decoded, gate_W, gate_b):
    out = core(token_embeddings, splat_influences, decoded, gate_W, gate_b)
    return out, e4m3fn_bytes(out * Y_SCALE)

@@ -1,0 +1,292 @@
+from contextlib import ExitStack
+
+import concourse.mybir as mybir
+from concourse.masks import make_identity
+
+F32 = mybir.dt.float32
+BF16 = mybir.dt.bfloat16
+U32 = mybir.dt.uint32
+U8 = mybir.dt.uint8
+FP8 = mybir.dt.float8_e4m3fn
+FP8X4 = mybir.dt.float8_e4m3fn_x4
+ALU = mybir.AluOpType
+ACT = mybir.ActivationFunctionType
+
+P = 128
+D = 1024
+KS = 128
+H = 512
+NT = 32
+NP = 16
+NQ = 8
+Y_SCALE = 160.0
+CV = 352
+
+FLOPS = 2 * 4096 * 1024 * 1024 + 2 * 4096 * 128 * 1024
+
+
+def tile_splatinformationflow_pb_kernel(
+    tc, token_embeddings, splat_influences, decoded, gate_W, gate_b, out_0, out_1
+):
+    nc = tc.nc
+    x_v = token_embeddings.flatten_outer_dims().rearrange("(q p j) k -> q p j k", p=P, j=4)
+    i_v = splat_influences.flatten_outer_dims().rearrange("(q p j) k -> q p j k", p=P, j=4)
+    w_v = gate_W.rearrange("(g p j) n -> g p j n", p=P, j=4)
+    o0_v = out_0.flatten_outer_dims().rearrange("(q p j) d -> q j p d", p=P, j=4)
+    o1_v = out_1.flatten_outer_dims().rearrange("(q p j) d -> q p (j d)", p=P, j=4)
+
+    with ExitStack() as ctx:
+        consts = ctx.enter_context(tc.tile_pool(name="consts", bufs=1))
+        xin = ctx.enter_context(tc.tile_pool(name="xin", bufs=3))
+        prep = ctx.enter_context(tc.tile_pool(name="prep", bufs=3))
+        ep = ctx.enter_context(tc.tile_pool(name="ep", bufs=3))
+        psum_acc = ctx.enter_context(tc.psum_pool(name="psum_acc", bufs=3))
+        psum_flow = ctx.enter_context(tc.psum_pool(name="psum_flow", bufs=2))
+        psum_tr = ctx.enter_context(tc.psum_pool(name="psum_tr", bufs=3))
+        ctx.enter_context(tc.manual_schedule())
+
+        x_sb, inf_sb, dec_sb = {}, {}, {}
+        w_raw, w_grp, w_codes, w_scales = {}, {}, {}, {}
+        xt, it, grp, codes, scales, inf_t = {}, {}, {}, {}, {}, {}
+        acc, fl, pre, gate, o0, o1 = {}, {}, {}, {}, {}, {}
+
+        warm = consts.tile([P, 2], F32, name="warm")
+        ones = consts.tile([P, P], BF16, name="ones")
+        brow = consts.tile([P, D], BF16, name="brow")
+        bias_sb = consts.tile([P, D], F32, name="bias_sb")
+        ident_f = consts.tile([P, P], F32, name="ident_f")
+        ident_b = consts.tile([P, P], BF16, name="ident_b")
+        nc.vector.memset(warm[:, 0:1], 0.0)
+        nc.scalar.activation(out=warm[:, 1:2], in_=warm[:, 0:1], func=ACT.Sigmoid)
+        nc.vector.memset(brow[:], 0.0)
+        nc.vector.memset(ones[:], 1.0)
+        make_identity(nc, ident_f[:])
+        make_identity(nc, ident_b[:])
+
+        def load_x(q, j0, j1):
+            if q not in x_sb:
+                x_sb[q] = xin.tile([P, 4, D], BF16, name="x_sb", tag="x_sb")
+            nc.sync.dma_start(out=x_sb[q][:, j0:j1, :], in_=x_v[q, :, j0:j1, :])
+
+        def load_inf(q):
+            inf_sb[q] = xin.tile([P, 4, KS], BF16, name="inf_sb", tag="inf_sb")
+            nc.sync.dma_start(out=inf_sb[q][:], in_=i_v[q])
+
+        def load_dec(b):
+            dec_sb[b] = consts.tile([P, D], BF16, name="dec%d" % b)
+            nc.sync.dma_start(out=dec_sb[b][:], in_=decoded[b])
+
+        def load_w(g, h):
+            w_raw[g, h] = consts.tile([P, 4, H], BF16, name="w_raw%d%d" % (g, h))
+            nc.sync.dma_start(out=w_raw[g, h][:], in_=w_v[g, :, :, h * H : (h + 1) * H])
+
+        def load_group(q):
+            load_x(q, 0, 4)
+            load_inf(q)
+            if q % 2 == 0:
+                load_dec(q // 2)
+
+        def w_interleave(g, h):
+            w_grp[g, h] = consts.tile([P, H, 4], BF16, name="w_grp%d%d" % (g, h), align_bytes=64)
+            nc.vector.tensor_copy(
+                out=w_grp[g, h][:, 0:CV, :], in_=w_raw[g, h][:, :, 0:CV].rearrange("p j c -> p c j")
+            )
+            nc.scalar.copy(
+                out=w_grp[g, h][:, CV:H, :], in_=w_raw[g, h][:, :, CV:H].rearrange("p j c -> p c j")
+            )
+
+        def w_quantize(g, h):
+            w_codes[g, h] = consts.tile([P, H], U32, name="w_codes%d%d" % (g, h), align_bytes=64)
+            w_scales[g, h] = consts.tile([P, H], U8, name="w_scales%d%d" % (g, h), align_bytes=64)
+            nc.vector.quantize_mx(
+                out=w_codes[g, h][:].bitcast(FP8X4),
+                scales=w_scales[g, h][:],
+                in_=w_grp[g, h][:].rearrange("p c j -> p (c j)"),
+            )
+
+        def bias_matmul():
+            for h in range(2):
+                acc["b", h] = psum_acc.tile([P, H], F32, name="acc", tag="acc")
+                nc.tensor.matmul(
+                    out=acc["b", h][:], lhsT=ones[:], rhs=brow[:, h * H : (h + 1) * H], start=True, stop=True
+                )
+
+        def bias_copy():
+            for h in range(2):
+                nc.scalar.copy(out=bias_sb[:, h * H : (h + 1) * H], in_=acc["b", h][:])
+
+        def transposes(pr):
+            q, j0 = pr // 2, 2 * (pr % 2)
+            words = x_sb[q][:].rearrange("p j k -> p (j k)").bitcast(F32)
+            for g in range(2):
+                xt[pr, g] = psum_tr.tile([P, 2, 2, P], F32, name="tr", tag="tr")
+                for jj in range(2):
+                    for u in range(2):
+                        w0 = (j0 + jj) * (D // 2) + g * 256
+                        nc.tensor.transpose(xt[pr, g][:, jj, u, :], words[:, w0 + u : w0 + 256 : 2], ident_f[:])
+            it[pr] = psum_tr.tile([P, 2, P], BF16, name="tr", tag="tr")
+            for jj in range(2):
+                nc.tensor.transpose(it[pr][:, jj, :], inf_sb[q][:, j0 + jj, :], ident_b[:])
+
+        def copy_x(pr, g, on_vector):
+            if g == 0:
+                grp[pr] = prep.tile([P, 2, 2 * P, 4], BF16, name="grp", tag="grp", align_bytes=64)
+            dst = grp[pr][:].rearrange("p g c t -> p (g c t)").bitcast(F32)[:, g * H : (g + 1) * H]
+            dst = dst.rearrange("p (jj r u) -> p jj r u", jj=2, u=2)
+            src = xt[pr, g][:].rearrange("p jj u r -> p jj r u")
+            if on_vector:
+                nc.vector.tensor_copy(out=dst, in_=src)
+            else:
+                nc.scalar.copy(out=dst, in_=src)
+
+        def copy_inf(pr):
+            inf_t[pr] = prep.tile([P, 2 * P], BF16, name="inf_t", tag="inf_t", bufs=4)
+            nc.scalar.copy(out=inf_t[pr][:], in_=it[pr][:].rearrange("p a b -> p (a b)"))
+
+        def quantize(pr):
+            codes[pr] = prep.tile([P, H], U32, name="codes", tag="codes", align_bytes=64)
+            scales[pr] = prep.tile([P, H], U8, name="scales", tag="scales", align_bytes=64)
+            nc.vector.quantize_mx(
+                out=codes[pr][:].bitcast(FP8X4),
+                scales=scales[pr][:],
+                in_=grp[pr][:].rearrange("p g c t -> p (g c t)"),
+            )
+
+        def gate_matmuls(s):
+            pr, jj = s // 2, s % 2
+            for h in range(2):
+                acc[s, h] = psum_acc.tile([P, H], F32, name="acc", tag="acc")
+                for g in range(2):
+                    cols = slice(g * 2 * P + jj * P, g * 2 * P + (jj + 1) * P)
+                    nc.tensor.matmul_mx(
+                        out=acc[s, h][:],
+                        lhsT=codes[pr][:, cols].bitcast(FP8X4),
+                        lhsT_scale=scales[pr][:, cols],
+                        rhs=w_codes[g, h][:].bitcast(FP8X4),
+                        rhs_scale=w_scales[g, h][:],
+                        start=(g == 0),
+                        stop=(g == 1),
+                    )
+
+        def flow_matmuls(s):
+            pr, jj = s // 2, s % 2
+            for h in range(2):
+                fl[s, h] = psum_flow.tile([P, H], F32, name="fl", tag="fl")
+                nc.tensor.matmul(
+                    out=fl[s, h][:],
+                    lhsT=inf_t[pr][:, jj * P : (jj + 1) * P],
+                    rhs=dec_sb[s // 8][:, h * H : (h + 1) * H],
+                    start=True,
+                    stop=True,
+                )
+
+        def add_bias(s):
+            pre[s] = ep.tile([P, D], F32, name="pre", tag="pre")
+            for h in range(2):
+                hs = slice(h * H, (h + 1) * H)
+                nc.vector.tensor_tensor(out=pre[s][:, hs], in0=acc[s, h][:], in1=bias_sb[:, hs], op=ALU.add)
+
+        def sigmoid(s):
+            gate[s] = ep.tile([P, D], F32, name="gate", tag="gate")
+            nc.scalar.activation(out=gate[s][:], in_=pre[s][:], func=ACT.Sigmoid)
+
+        def product(s, h):
+            if h == 0:
+                o0[s] = ep.tile([P, D], F32, name="o0", tag="o0", bufs=6)
+            hs = slice(h * H, (h + 1) * H)
+            nc.vector.tensor_tensor(out=o0[s][:, hs], in0=fl[s, h][:], in1=gate[s][:, hs], op=ALU.mult)
+
+        def cast(s, c0, c1):
+            q, j = s // 4, s % 4
+            if j == 0 and c0 == 0:
+                o1[q] = ep.tile([P, 4, D], FP8, name="o1", tag="o1")
+            nc.scalar.activation(
+                out=o1[q][:, j, c0:c1], in_=o0[s][:, c0:c1], func=ACT.Copy, scale=Y_SCALE, saturate=False
+            )
+
+        def store_o0(s, c0, c1):
+            nc.sync.dma_start(out=o0_v[s // 4, s % 4, :, c0:c1], in_=o0[s][:, c0:c1])
+
+        def store_o1(q, j0, j1):
+            nc.sync.dma_start(
+                out=o1_v[q, :, j0 * D : j1 * D],
+                in_=o1[q][:, j0:j1, :].rearrange("p j d -> p (j d)").bitcast(U8),
+            )
+
+        def finish(s):
+            q, j = s // 4, s % 4
+            if s < NT - 1:
+                product(s, 0)
+                product(s, 1)
+                store_o0(s, 0, D)
+            else:
+                for h in range(2):
+                    product(s, h)
+                    store_o0(s, h * H, (h + 1) * H)
+
+        def finish_bytes(s):
+            q, j = s // 4, s % 4
+            if s < NT - 1:
+                cast(s, 0, D)
+                if j == 3:
+                    store_o1(q, 0, 4)
+                if s == NT - 2:
+                    store_o1(q, 0, 3)
+            else:
+                cast(s, 0, H)
+                cast(s, H, D)
+                store_o1(q, 3, 4)
+
+        load_x(0, 0, 2)
+        load_inf(0)
+        nc.sync.dma_start(out=brow[0:1, :], in_=gate_b.rearrange("(o n) -> o n", o=1))
+        load_w(0, 0)
+        load_w(1, 0)
+        load_x(0, 2, 4)
+        load_w(0, 1)
+        load_w(1, 1)
+        load_dec(0)
+        load_x(1, 0, 4)
+        load_inf(1)
+
+        for s in range(-4, NT + 1):
+            if s >= 0 and s % 4 == 0 and s // 4 + 2 < NQ:
+                load_group(s // 4 + 2)
+            if 0 <= s < NT:
+                gate_matmuls(s)
+            if 0 <= s - 1 < NT:
+                flow_matmuls(s - 1)
+            if 0 <= s < NT:
+                add_bias(s)
+            if s == -3:
+                w_interleave(0, 0)
+            if s == -2:
+                w_interleave(1, 0)
+                w_quantize(0, 0)
+            if s == -1:
+                w_quantize(1, 0)
+            if (s + 1) % 2 == 0 and 0 <= (s + 1) // 2 < NP:
+                quantize((s + 1) // 2)
+            if 0 <= s - 1 < NT:
+                finish(s - 1)
+            if (s + 3) % 2 == 0 and 0 <= (s + 3) // 2 < NP:
+                copy_x((s + 3) // 2, 0, False)
+            if (s + 2) % 2 == 0 and 0 <= (s + 2) // 2 < NP:
+                pr = (s + 2) // 2
+                copy_x(pr, 1, pr % 2 == 1 and pr > 1)
+                copy_inf(pr)
+            if s == -2:
+                bias_copy()
+            if s == -1:
+                w_interleave(0, 1)
+                w_interleave(1, 1)
+                w_quantize(0, 1)
+                w_quantize(1, 1)
+            if 0 <= s < NT:
+                sigmoid(s)
+            if 0 <= s - 1 < NT:
+                finish_bytes(s - 1)
+            if (s + 4) % 2 == 0 and 0 <= (s + 4) // 2 < NP:
+                transposes((s + 4) // 2)
+            if s == -4:
+                bias_matmul()

@@ -20,7 +20,7 @@ NT = 32
 NP = 16
 NQ = 8
 Y_SCALE = 160.0
-CV = 352
+CV = 256
 
 FLOPS = 2 * 4096 * 1024 * 1024 + 2 * 4096 * 128 * 1024
 
@@ -204,6 +204,11 @@ def tile_splatinformationflow_pb_kernel(
                 out=o1[q][:, j, c0:c1], in_=o0[s][:, c0:c1], func=ACT.Copy, scale=Y_SCALE, saturate=False
             )
 
+        def cast_on_vector(s):
+            nc.vector.tensor_scalar(
+                out=o1[s // 4][:, s % 4, :], in0=o0[s][:], scalar1=Y_SCALE, scalar2=None, op0=ALU.mult, saturate=False
+            )
+
         def store_o0(s, c0, c1):
             nc.sync.dma_start(out=o0_v[s // 4, s % 4, :, c0:c1], in_=o0[s][:, c0:c1])
 
@@ -227,7 +232,8 @@ def tile_splatinformationflow_pb_kernel(
         def finish_bytes(s):
             q, j = s // 4, s % 4
             if s < NT - 1:
-                cast(s, 0, D)
+                if j != 1:
+                    cast(s, 0, D)
                 if j == 3:
                     store_o1(q, 0, 4)
                 if s == NT - 2:
@@ -237,56 +243,64 @@ def tile_splatinformationflow_pb_kernel(
                 cast(s, H, D)
                 store_o1(q, 3, 4)
 
+        for h in range(2):
+            for g in range(2):
+                load_w(g, h)
         load_x(0, 0, 2)
         load_inf(0)
         nc.sync.dma_start(out=brow[0:1, :], in_=gate_b.rearrange("(o n) -> o n", o=1))
-        load_w(0, 0)
-        load_w(1, 0)
         load_x(0, 2, 4)
-        load_w(0, 1)
-        load_w(1, 1)
         load_dec(0)
         load_x(1, 0, 4)
         load_inf(1)
+        w_interleave(0, 0)
+        w_interleave(1, 0)
+        w_quantize(0, 0)
+        w_interleave(0, 1)
+        w_quantize(1, 0)
+        w_interleave(1, 1)
+        w_quantize(0, 1)
+        w_quantize(1, 1)
+
+        def pair_at(s, lead):
+            if (s + lead) % 2 == 0 and 0 <= (s + lead) // 2 < NP:
+                return (s + lead) // 2
+            return None
+
+        def on_vector(pr):
+            return False
 
         for s in range(-4, NT + 1):
             if s >= 0 and s % 4 == 0 and s // 4 + 2 < NQ:
                 load_group(s // 4 + 2)
+            pr_t, pr_x1, pr_q = pair_at(s, 4), pair_at(s, 3), pair_at(s, 2)
             if 0 <= s < NT:
                 gate_matmuls(s)
+            if pr_t is not None:
+                transposes(pr_t)
+            if s == -4:
+                bias_matmul()
             if 0 <= s - 1 < NT:
                 flow_matmuls(s - 1)
+            if pr_t is not None:
+                copy_x(pr_t, 0, False)
+            if pr_x1 is not None:
+                if not on_vector(pr_x1):
+                    copy_x(pr_x1, 1, False)
+                copy_inf(pr_x1)
+            if s == -3:
+                bias_copy()
             if 0 <= s < NT:
                 add_bias(s)
-            if s == -3:
-                w_interleave(0, 0)
-            if s == -2:
-                w_interleave(1, 0)
-                w_quantize(0, 0)
-            if s == -1:
-                w_quantize(1, 0)
-            if (s + 1) % 2 == 0 and 0 <= (s + 1) // 2 < NP:
-                quantize((s + 1) // 2)
-            if 0 <= s - 1 < NT:
-                finish(s - 1)
-            if (s + 3) % 2 == 0 and 0 <= (s + 3) // 2 < NP:
-                copy_x((s + 3) // 2, 0, False)
-            if (s + 2) % 2 == 0 and 0 <= (s + 2) // 2 < NP:
-                pr = (s + 2) // 2
-                copy_x(pr, 1, pr % 2 == 1 and pr > 1)
-                copy_inf(pr)
-            if s == -2:
-                bias_copy()
-            if s == -1:
-                w_interleave(0, 1)
-                w_interleave(1, 1)
-                w_quantize(0, 1)
-                w_quantize(1, 1)
+            if pr_q is not None:
+                quantize(pr_q)
+            if 0 <= s - 2 < NT and (s - 2) % 4 == 1:
+                cast_on_vector(s - 2)
             if 0 <= s < NT:
                 sigmoid(s)
             if 0 <= s - 1 < NT:
+                finish(s - 1)
+            if pr_x1 is not None and on_vector(pr_x1):
+                copy_x(pr_x1, 1, True)
+            if 0 <= s - 1 < NT:
                 finish_bytes(s - 1)
-            if (s + 4) % 2 == 0 and 0 <= (s + 4) // 2 < NP:
-                transposes((s + 4) // 2)
-            if s == -4:
-                bias_matmul()

@@ -204,10 +204,18 @@ def tile_splatinformationflow_pb_kernel(
                 out=o1[q][:, j, c0:c1], in_=o0[s][:, c0:c1], func=ACT.Copy, scale=Y_SCALE, saturate=False
             )
 
-        def cast_on_vector(s):
-            nc.vector.tensor_scalar(
-                out=o1[s // 4][:, s % 4, :], in0=o0[s][:], scalar1=Y_SCALE, scalar2=None, op0=ALU.mult, saturate=False
+        def shares_cast(s):
+            return s % 2 == 1 and s < NT - 1
+
+        def cast_on_gpsimd(s):
+            scaled = ep.tile([P, H], F32, name="scaled", tag="scaled")
+            nc.gpsimd.tensor_scalar(
+                out=scaled[:], in0=o0[s][:, 0:H], scalar1=Y_SCALE, scalar2=0.0, op0=ALU.mult, op1=ALU.add
             )
+            for c0 in range(0, H, H // 2):
+                nc.gpsimd.tensor_copy(
+                    out=o1[s // 4][:, s % 4, c0 : c0 + H // 2], in_=scaled[:, c0 : c0 + H // 2], saturate=False
+                )
 
         def store_o0(s, c0, c1):
             nc.sync.dma_start(out=o0_v[s // 4, s % 4, :, c0:c1], in_=o0[s][:, c0:c1])
@@ -232,7 +240,9 @@ def tile_splatinformationflow_pb_kernel(
         def finish_bytes(s):
             q, j = s // 4, s % 4
             if s < NT - 1:
-                if j != 1:
+                if shares_cast(s):
+                    cast(s, H, D)
+                else:
                     cast(s, 0, D)
                 if j == 3:
                     store_o1(q, 0, 4)
@@ -294,12 +304,12 @@ def tile_splatinformationflow_pb_kernel(
                 add_bias(s)
             if pr_q is not None:
                 quantize(pr_q)
-            if 0 <= s - 2 < NT and (s - 2) % 4 == 1:
-                cast_on_vector(s - 2)
             if 0 <= s < NT:
                 sigmoid(s)
             if 0 <= s - 1 < NT:
                 finish(s - 1)
+                if shares_cast(s - 1):
+                    cast_on_gpsimd(s - 1)
             if pr_x1 is not None and on_vector(pr_x1):
                 copy_x(pr_x1, 1, True)
             if 0 <= s - 1 < NT:

@@ -20,7 +20,7 @@ NT = 32
 NP = 16
 NQ = 8
 Y_SCALE = 160.0
-CV = 256
+CV = 352
 
 FLOPS = 2 * 4096 * 1024 * 1024 + 2 * 4096 * 128 * 1024
 
@@ -60,6 +60,8 @@ def tile_splatinformationflow_pb_kernel(
         nc.scalar.activation(out=warm[:, 1:2], in_=warm[:, 0:1], func=ACT.Sigmoid)
         nc.vector.memset(brow[:], 0.0)
         nc.vector.memset(ones[:], 1.0)
+        idle_rhs = consts.tile([P, H], BF16, name="idle_rhs")
+        nc.gpsimd.memset(idle_rhs[:], 0.0)
         make_identity(nc, ident_f[:])
         make_identity(nc, ident_b[:])
 
@@ -110,6 +112,11 @@ def tile_splatinformationflow_pb_kernel(
                 nc.tensor.matmul(
                     out=acc["b", h][:], lhsT=ones[:], rhs=brow[:, h * H : (h + 1) * H], start=True, stop=True
                 )
+
+        def keep_tensor_busy(n):
+            idle_out = psum_flow.tile([P, H], F32, name="fl", tag="fl")
+            for i in range(n):
+                nc.tensor.matmul(out=idle_out[:], lhsT=ones[:], rhs=idle_rhs[:], start=True, stop=True)
 
         def bias_copy():
             for h in range(2):
@@ -188,7 +195,9 @@ def tile_splatinformationflow_pb_kernel(
 
         def sigmoid(s):
             gate[s] = ep.tile([P, D], F32, name="gate", tag="gate")
-            nc.scalar.activation(out=gate[s][:], in_=pre[s][:], func=ACT.Sigmoid)
+            width = D if s < NT - 1 else H
+            for c0 in range(0, D, width):
+                nc.scalar.activation(out=gate[s][:, c0 : c0 + width], in_=pre[s][:, c0 : c0 + width], func=ACT.Sigmoid)
 
         def product(s, h):
             if h == 0:
@@ -253,24 +262,37 @@ def tile_splatinformationflow_pb_kernel(
                 cast(s, H, D)
                 store_o1(q, 3, 4)
 
-        for h in range(2):
-            for g in range(2):
-                load_w(g, h)
+        load_w(0, 0)
         load_x(0, 0, 2)
         load_inf(0)
+        load_w(1, 0)
+        load_w(0, 1)
+        load_w(1, 1)
         nc.sync.dma_start(out=brow[0:1, :], in_=gate_b.rearrange("(o n) -> o n", o=1))
         load_x(0, 2, 4)
-        load_dec(0)
         load_x(1, 0, 4)
         load_inf(1)
+        load_dec(0)
         w_interleave(0, 0)
-        w_interleave(1, 0)
+        transposes(0)
+        keep_tensor_busy(8)
+        copy_x(0, 0, False)
+        copy_x(0, 1, False)
+        copy_inf(0)
         w_quantize(0, 0)
+        w_interleave(1, 0)
+        quantize(0)
         w_interleave(0, 1)
         w_quantize(1, 0)
         w_interleave(1, 1)
         w_quantize(0, 1)
         w_quantize(1, 1)
+        bias_matmul()
+        bias_copy()
+        transposes(1)
+        copy_x(1, 0, False)
+        copy_x(1, 1, False)
+        copy_inf(1)
 
         def pair_at(s, lead):
             if (s + lead) % 2 == 0 and 0 <= (s + lead) // 2 < NP:
@@ -280,7 +302,7 @@ def tile_splatinformationflow_pb_kernel(
         def on_vector(pr):
             return False
 
-        for s in range(-4, NT + 1):
+        for s in range(0, NT + 1):
             if s >= 0 and s % 4 == 0 and s // 4 + 2 < NQ:
                 load_group(s // 4 + 2)
             pr_t, pr_x1, pr_q = pair_at(s, 4), pair_at(s, 3), pair_at(s, 2)
@@ -288,8 +310,6 @@ def tile_splatinformationflow_pb_kernel(
                 gate_matmuls(s)
             if pr_t is not None:
                 transposes(pr_t)
-            if s == -4:
-                bias_matmul()
             if 0 <= s - 1 < NT:
                 flow_matmuls(s - 1)
             if pr_t is not None:
@@ -298,8 +318,6 @@ def tile_splatinformationflow_pb_kernel(
                 if not on_vector(pr_x1):
                     copy_x(pr_x1, 1, False)
                 copy_inf(pr_x1)
-            if s == -3:
-                bias_copy()
             if 0 <= s < NT:
                 add_bias(s)
             if pr_q is not None:

@@ -21,6 +21,7 @@ NP = 16
 NQ = 8
 Y_SCALE = 160.0
 CV = 352
+GC = 640
 
 FLOPS = 2 * 4096 * 1024 * 1024 + 2 * 4096 * 128 * 1024
 
@@ -217,14 +218,13 @@ def tile_splatinformationflow_pb_kernel(
             return s % 2 == 1 and s < NT - 1
 
         def cast_on_gpsimd(s):
-            scaled = ep.tile([P, H], F32, name="scaled", tag="scaled")
-            nc.gpsimd.tensor_scalar(
-                out=scaled[:], in0=o0[s][:, 0:H], scalar1=Y_SCALE, scalar2=0.0, op0=ALU.mult, op1=ALU.add
-            )
-            for c0 in range(0, H, H // 2):
-                nc.gpsimd.tensor_copy(
-                    out=o1[s // 4][:, s % 4, c0 : c0 + H // 2], in_=scaled[:, c0 : c0 + H // 2], saturate=False
+            scaled = ep.tile([P, GC], F32, name="scaled", tag="scaled")
+            for c0, c1 in ((0, H), (H, GC)):
+                nc.gpsimd.tensor_scalar(
+                    out=scaled[:, c0:c1], in0=o0[s][:, c0:c1], scalar1=Y_SCALE, scalar2=0.0, op0=ALU.mult, op1=ALU.add
                 )
+            for c0, c1 in ((0, H // 2), (H // 2, H), (H, GC)):
+                nc.gpsimd.tensor_copy(out=o1[s // 4][:, s % 4, c0:c1], in_=scaled[:, c0:c1], saturate=False)
 
         def store_o0(s, c0, c1):
             nc.sync.dma_start(out=o0_v[s // 4, s % 4, :, c0:c1], in_=o0[s][:, c0:c1])
@@ -250,7 +250,7 @@ def tile_splatinformationflow_pb_kernel(
             q, j = s // 4, s % 4
             if s < NT - 1:
                 if shares_cast(s):
-                    cast(s, H, D)
+                    cast(s, GC, D)
                 else:
                     cast(s, 0, D)
                 if j == 3:

@@ -79,9 +79,9 @@ def tile_splatinformationflow_pb_kernel(
             dec_sb[b] = consts.tile([P, D], BF16, name="dec%d" % b)
             nc.sync.dma_start(out=dec_sb[b][:], in_=decoded[b])
 
-        def load_w(g, h):
-            w_raw[g, h] = consts.tile([P, 4, H], BF16, name="w_raw%d%d" % (g, h))
-            nc.sync.dma_start(out=w_raw[g, h][:], in_=w_v[g, :, :, h * H : (h + 1) * H])
+        def load_w(g):
+            w_raw[g] = consts.tile([P, 4, D], BF16, name="w_raw%d" % g)
+            nc.sync.dma_start(out=w_raw[g][:], in_=w_v[g])
 
         def load_group(q):
             load_x(q, 0, 4)
@@ -91,11 +91,12 @@ def tile_splatinformationflow_pb_kernel(
 
         def w_interleave(g, h):
             w_grp[g, h] = consts.tile([P, H, 4], BF16, name="w_grp%d%d" % (g, h), align_bytes=64)
+            c0 = h * H
             nc.vector.tensor_copy(
-                out=w_grp[g, h][:, 0:CV, :], in_=w_raw[g, h][:, :, 0:CV].rearrange("p j c -> p c j")
+                out=w_grp[g, h][:, 0:CV, :], in_=w_raw[g][:, :, c0 : c0 + CV].rearrange("p j c -> p c j")
             )
             nc.scalar.copy(
-                out=w_grp[g, h][:, CV:H, :], in_=w_raw[g, h][:, :, CV:H].rearrange("p j c -> p c j")
+                out=w_grp[g, h][:, CV:H, :], in_=w_raw[g][:, :, c0 + CV : c0 + H].rearrange("p j c -> p c j")
             )
 
         def w_quantize(g, h):
@@ -262,30 +263,28 @@ def tile_splatinformationflow_pb_kernel(
                 cast(s, H, D)
                 store_o1(q, 3, 4)
 
-        load_w(0, 0)
+        load_w(0)
         load_x(0, 0, 2)
         load_inf(0)
-        load_w(1, 0)
-        load_w(0, 1)
-        load_w(1, 1)
+        load_w(1)
         nc.sync.dma_start(out=brow[0:1, :], in_=gate_b.rearrange("(o n) -> o n", o=1))
         load_x(0, 2, 4)
         load_x(1, 0, 4)
         load_inf(1)
         load_dec(0)
-        w_interleave(0, 0)
-        transposes(0)
         keep_tensor_busy(8)
+        w_interleave(0, 0)
+        w_interleave(0, 1)
+        transposes(0)
+        w_quantize(0, 0)
         copy_x(0, 0, False)
         copy_x(0, 1, False)
         copy_inf(0)
-        w_quantize(0, 0)
-        w_interleave(1, 0)
-        quantize(0)
-        w_interleave(0, 1)
-        w_quantize(1, 0)
-        w_interleave(1, 1)
         w_quantize(0, 1)
+        quantize(0)
+        w_interleave(1, 0)
+        w_interleave(1, 1)
+        w_quantize(1, 0)
         w_quantize(1, 1)
         bias_matmul()
         bias_copy()

@@ -21,7 +21,7 @@ NP = 16
 NQ = 8
 Y_SCALE = 160.0
 CV = 352
-GC = 640
+GC = 768
 
 FLOPS = 2 * 4096 * 1024 * 1024 + 2 * 4096 * 128 * 1024
 

@@ -22,6 +22,7 @@ NQ = 8
 Y_SCALE = 160.0
 CV = 352
 GC = 768
+GP = 128
 
 FLOPS = 2 * 4096 * 1024 * 1024 + 2 * 4096 * 128 * 1024
 
@@ -41,15 +42,16 @@ def tile_splatinformationflow_pb_kernel(
         xin = ctx.enter_context(tc.tile_pool(name="xin", bufs=3))
         prep = ctx.enter_context(tc.tile_pool(name="prep", bufs=3))
         ep = ctx.enter_context(tc.tile_pool(name="ep", bufs=3))
-        psum_acc = ctx.enter_context(tc.psum_pool(name="psum_acc", bufs=3))
+        psum_acc = ctx.enter_context(tc.psum_pool(name="psum_acc", bufs=2))
         psum_flow = ctx.enter_context(tc.psum_pool(name="psum_flow", bufs=2))
+        psum_side = ctx.enter_context(tc.psum_pool(name="psum_side", bufs=1))
         psum_tr = ctx.enter_context(tc.psum_pool(name="psum_tr", bufs=3))
         ctx.enter_context(tc.manual_schedule())
 
         x_sb, inf_sb, dec_sb = {}, {}, {}
         w_raw, w_grp, w_codes, w_scales = {}, {}, {}, {}
         xt, it, grp, codes, scales, inf_t = {}, {}, {}, {}, {}, {}
-        acc, fl, pre, gate, o0, o1 = {}, {}, {}, {}, {}, {}
+        acc, fl, pre, gate, o0, o1, fl_side, fl_sb, scaled = {}, {}, {}, {}, {}, {}, {}, {}, {}
 
         warm = consts.tile([P, 2], F32, name="warm")
         ones = consts.tile([P, P], BF16, name="ones")
@@ -177,17 +179,32 @@ def tile_splatinformationflow_pb_kernel(
                         stop=(g == 1),
                     )
 
+        def shares_product(s):
+            return s % 2 == 0 and s < NT - 2
+
         def flow_matmuls(s):
             pr, jj = s // 2, s % 2
+            lhsT = inf_t[pr][:, jj * P : (jj + 1) * P]
             for h in range(2):
+                width = H - GP if h == 1 and shares_product(s) else H
                 fl[s, h] = psum_flow.tile([P, H], F32, name="fl", tag="fl")
                 nc.tensor.matmul(
-                    out=fl[s, h][:],
-                    lhsT=inf_t[pr][:, jj * P : (jj + 1) * P],
-                    rhs=dec_sb[s // 8][:, h * H : (h + 1) * H],
+                    out=fl[s, h][:, 0:width],
+                    lhsT=lhsT,
+                    rhs=dec_sb[s // 8][:, h * H : h * H + width],
                     start=True,
                     stop=True,
                 )
+            if shares_product(s):
+                fl_side[s] = psum_side.tile([P, GP], F32, name="fl_side", tag="fl_side")
+                nc.tensor.matmul(out=fl_side[s][:], lhsT=lhsT, rhs=dec_sb[s // 8][:, D - GP : D], start=True, stop=True)
+
+        def copy_flow(s):
+            fl_sb[s] = ep.tile([P, GP], F32, name="fl_sb", tag="fl_sb")
+            nc.scalar.copy(out=fl_sb[s][:], in_=fl_side[s][:])
+
+        def product_on_gpsimd(s):
+            nc.gpsimd.tensor_tensor(out=o0[s][:, D - GP : D], in0=fl_sb[s][:], in1=gate[s][:, D - GP : D], op=ALU.mult)
 
         def add_bias(s):
             pre[s] = ep.tile([P, D], F32, name="pre", tag="pre")
@@ -204,8 +221,9 @@ def tile_splatinformationflow_pb_kernel(
         def product(s, h):
             if h == 0:
                 o0[s] = ep.tile([P, D], F32, name="o0", tag="o0", bufs=6)
-            hs = slice(h * H, (h + 1) * H)
-            nc.vector.tensor_tensor(out=o0[s][:, hs], in0=fl[s, h][:], in1=gate[s][:, hs], op=ALU.mult)
+            width = H - GP if h == 1 and shares_product(s) else H
+            hs = slice(h * H, h * H + width)
+            nc.vector.tensor_tensor(out=o0[s][:, hs], in0=fl[s, h][:, 0:width], in1=gate[s][:, hs], op=ALU.mult)
 
         def cast(s, c0, c1):
             q, j = s // 4, s % 4
@@ -218,14 +236,20 @@ def tile_splatinformationflow_pb_kernel(
         def shares_cast(s):
             return s % 2 == 1 and s < NT - 1
 
-        def cast_on_gpsimd(s):
-            scaled = ep.tile([P, GC], F32, name="scaled", tag="scaled")
+        def gpsimd_casts(s, pieces):
+            for c0, c1 in pieces:
+                nc.gpsimd.tensor_copy(out=o1[s // 4][:, s % 4, c0:c1], in_=scaled[s][:, c0:c1], saturate=False)
+
+        def cast_on_gpsimd_first(s):
+            scaled[s] = ep.tile([P, GC], F32, name="scaled", tag="scaled")
             for c0, c1 in ((0, H), (H, GC)):
                 nc.gpsimd.tensor_scalar(
-                    out=scaled[:, c0:c1], in0=o0[s][:, c0:c1], scalar1=Y_SCALE, scalar2=0.0, op0=ALU.mult, op1=ALU.add
+                    out=scaled[s][:, c0:c1], in0=o0[s][:, c0:c1], scalar1=Y_SCALE, scalar2=0.0, op0=ALU.mult, op1=ALU.add
                 )
-            for c0, c1 in ((0, H // 2), (H // 2, H), (H, GC)):
-                nc.gpsimd.tensor_copy(out=o1[s // 4][:, s % 4, c0:c1], in_=scaled[:, c0:c1], saturate=False)
+            gpsimd_casts(s, ((0, H // 2),))
+
+        def cast_on_gpsimd_rest(s):
+            gpsimd_casts(s, ((H // 2, H), (H, GC)))
 
         def store_o0(s, c0, c1):
             nc.sync.dma_start(out=o0_v[s // 4, s % 4, :, c0:c1], in_=o0[s][:, c0:c1])
@@ -241,6 +265,8 @@ def tile_splatinformationflow_pb_kernel(
             if s < NT - 1:
                 product(s, 0)
                 product(s, 1)
+                if shares_product(s):
+                    product_on_gpsimd(s)
                 store_o0(s, 0, D)
             else:
                 for h in range(2):
@@ -254,8 +280,6 @@ def tile_splatinformationflow_pb_kernel(
                     cast(s, GC, D)
                 else:
                     cast(s, 0, D)
-                if j == 3:
-                    store_o1(q, 0, 4)
                 if s == NT - 2:
                     store_o1(q, 0, 3)
             else:
@@ -311,6 +335,8 @@ def tile_splatinformationflow_pb_kernel(
                 transposes(pr_t)
             if 0 <= s - 1 < NT:
                 flow_matmuls(s - 1)
+                if shares_product(s - 1):
+                    copy_flow(s - 1)
             if pr_t is not None:
                 copy_x(pr_t, 0, False)
             if pr_x1 is not None:
@@ -326,7 +352,11 @@ def tile_splatinformationflow_pb_kernel(
             if 0 <= s - 1 < NT:
                 finish(s - 1)
                 if shares_cast(s - 1):
-                    cast_on_gpsimd(s - 1)
+                    cast_on_gpsimd_first(s - 1)
+                if s - 2 >= 0 and shares_cast(s - 2):
+                    cast_on_gpsimd_rest(s - 2)
+                    if (s - 2) % 4 == 3:
+                        store_o1((s - 2) // 4, 0, 4)
             if pr_x1 is not None and on_vector(pr_x1):
                 copy_x(pr_x1, 1, True)
             if 0 <= s - 1 < NT:

@@ -21,8 +21,8 @@ NP = 16
 NQ = 8
 Y_SCALE = 160.0
 CV = 352
-GC = 768
-GP = 128
+GC = 960
+GP = 192
 
 FLOPS = 2 * 4096 * 1024 * 1024 + 2 * 4096 * 128 * 1024
 
@@ -246,10 +246,10 @@ def tile_splatinformationflow_pb_kernel(
                 nc.gpsimd.tensor_scalar(
                     out=scaled[s][:, c0:c1], in0=o0[s][:, c0:c1], scalar1=Y_SCALE, scalar2=0.0, op0=ALU.mult, op1=ALU.add
                 )
-            gpsimd_casts(s, ((0, H // 2),))
+            gpsimd_casts(s, ((0, H),))
 
         def cast_on_gpsimd_rest(s):
-            gpsimd_casts(s, ((H // 2, H), (H, GC)))
+            gpsimd_casts(s, ((H, GC),))
 
         def store_o0(s, c0, c1):
             nc.sync.dma_start(out=o0_v[s // 4, s % 4, :, c0:c1], in_=o0[s][:, c0:c1])

from contextlib import ExitStack

import concourse.mybir as mybir
from concourse.masks import make_identity

F32 = mybir.dt.float32
BF16 = mybir.dt.bfloat16
U32 = mybir.dt.uint32
U8 = mybir.dt.uint8
FP8 = mybir.dt.float8_e4m3fn
FP8X4 = mybir.dt.float8_e4m3fn_x4
ALU = mybir.AluOpType
ACT = mybir.ActivationFunctionType

P = 128
D = 1024
KS = 128
H = 512
NT = 32
NP = 16
NQ = 8
Y_SCALE = 160.0
CV = 352
GC = 960
GP = 192

FLOPS = 2 * 4096 * 1024 * 1024 + 2 * 4096 * 128 * 1024


def tile_splatinformationflow_pb_kernel(
    tc, token_embeddings, splat_influences, decoded, gate_W, gate_b, out_0, out_1
):
    nc = tc.nc
    x_v = token_embeddings.flatten_outer_dims().rearrange("(q p j) k -> q p j k", p=P, j=4)
    i_v = splat_influences.flatten_outer_dims().rearrange("(q p j) k -> q p j k", p=P, j=4)
    w_v = gate_W.rearrange("(g p j) n -> g p j n", p=P, j=4)
    o0_v = out_0.flatten_outer_dims().rearrange("(q p j) d -> q j p d", p=P, j=4)
    o1_v = out_1.flatten_outer_dims().rearrange("(q p j) d -> q p (j d)", p=P, j=4)

    with ExitStack() as ctx:
        consts = ctx.enter_context(tc.tile_pool(name="consts", bufs=1))
        xin = ctx.enter_context(tc.tile_pool(name="xin", bufs=3))
        prep = ctx.enter_context(tc.tile_pool(name="prep", bufs=3))
        ep = ctx.enter_context(tc.tile_pool(name="ep", bufs=3))
        psum_acc = ctx.enter_context(tc.psum_pool(name="psum_acc", bufs=2))
        psum_flow = ctx.enter_context(tc.psum_pool(name="psum_flow", bufs=2))
        psum_side = ctx.enter_context(tc.psum_pool(name="psum_side", bufs=1))
        psum_tr = ctx.enter_context(tc.psum_pool(name="psum_tr", bufs=3))
        ctx.enter_context(tc.manual_schedule())

        x_sb, inf_sb, dec_sb = {}, {}, {}
        w_raw, w_grp, w_codes, w_scales = {}, {}, {}, {}
        xt, it, grp, codes, scales, inf_t = {}, {}, {}, {}, {}, {}
        acc, fl, pre, gate, o0, o1, fl_side, fl_sb, scaled = {}, {}, {}, {}, {}, {}, {}, {}, {}

        warm = consts.tile([P, 2], F32, name="warm")
        ones = consts.tile([P, P], BF16, name="ones")
        brow = consts.tile([P, D], BF16, name="brow")
        bias_sb = consts.tile([P, D], F32, name="bias_sb")
        ident_f = consts.tile([P, P], F32, name="ident_f")
        ident_b = consts.tile([P, P], BF16, name="ident_b")
        nc.vector.memset(warm[:, 0:1], 0.0)
        nc.scalar.activation(out=warm[:, 1:2], in_=warm[:, 0:1], func=ACT.Sigmoid)
        nc.vector.memset(brow[:], 0.0)
        nc.vector.memset(ones[:], 1.0)
        idle_rhs = consts.tile([P, H], BF16, name="idle_rhs")
        nc.gpsimd.memset(idle_rhs[:], 0.0)
        make_identity(nc, ident_f[:])
        make_identity(nc, ident_b[:])

        def load_x(q, j0, j1):
            if q not in x_sb:
                x_sb[q] = xin.tile([P, 4, D], BF16, name="x_sb", tag="x_sb")
            nc.sync.dma_start(out=x_sb[q][:, j0:j1, :], in_=x_v[q, :, j0:j1, :])

        def load_inf(q):
            inf_sb[q] = xin.tile([P, 4, KS], BF16, name="inf_sb", tag="inf_sb")
            nc.sync.dma_start(out=inf_sb[q][:], in_=i_v[q])

        def load_dec(b):
            dec_sb[b] = consts.tile([P, D], BF16, name="dec%d" % b)
            nc.sync.dma_start(out=dec_sb[b][:], in_=decoded[b])

        def load_w(g):
            w_raw[g] = consts.tile([P, 4, D], BF16, name="w_raw%d" % g)
            nc.sync.dma_start(out=w_raw[g][:], in_=w_v[g])

        def load_group(q):
            load_x(q, 0, 4)
            load_inf(q)
            if q % 2 == 0:
                load_dec(q // 2)

        def w_interleave(g, h):
            w_grp[g, h] = consts.tile([P, H, 4], BF16, name="w_grp%d%d" % (g, h), align_bytes=64)
            c0 = h * H
            nc.vector.tensor_copy(
                out=w_grp[g, h][:, 0:CV, :], in_=w_raw[g][:, :, c0 : c0 + CV].rearrange("p j c -> p c j")
            )
            nc.scalar.copy(
                out=w_grp[g, h][:, CV:H, :], in_=w_raw[g][:, :, c0 + CV : c0 + H].rearrange("p j c -> p c j")
            )

        def w_quantize(g, h):
            w_codes[g, h] = consts.tile([P, H], U32, name="w_codes%d%d" % (g, h), align_bytes=64)
            w_scales[g, h] = consts.tile([P, H], U8, name="w_scales%d%d" % (g, h), align_bytes=64)
            nc.vector.quantize_mx(
                out=w_codes[g, h][:].bitcast(FP8X4),
                scales=w_scales[g, h][:],
                in_=w_grp[g, h][:].rearrange("p c j -> p (c j)"),
            )

        def bias_matmul():
            for h in range(2):
                acc["b", h] = psum_acc.tile([P, H], F32, name="acc", tag="acc")
                nc.tensor.matmul(
                    out=acc["b", h][:], lhsT=ones[:], rhs=brow[:, h * H : (h + 1) * H], start=True, stop=True
                )

        def keep_tensor_busy(n):
            idle_out = psum_flow.tile([P, H], F32, name="fl", tag="fl")
            for i in range(n):
                nc.tensor.matmul(out=idle_out[:], lhsT=ones[:], rhs=idle_rhs[:], start=True, stop=True)

        def bias_copy():
            for h in range(2):
                nc.scalar.copy(out=bias_sb[:, h * H : (h + 1) * H], in_=acc["b", h][:])

        def transposes(pr):
            q, j0 = pr // 2, 2 * (pr % 2)
            words = x_sb[q][:].rearrange("p j k -> p (j k)").bitcast(F32)
            for g in range(2):
                xt[pr, g] = psum_tr.tile([P, 2, 2, P], F32, name="tr", tag="tr")
                for jj in range(2):
                    for u in range(2):
                        w0 = (j0 + jj) * (D // 2) + g * 256
                        nc.tensor.transpose(xt[pr, g][:, jj, u, :], words[:, w0 + u : w0 + 256 : 2], ident_f[:])
            it[pr] = psum_tr.tile([P, 2, P], BF16, name="tr", tag="tr")
            for jj in range(2):
                nc.tensor.transpose(it[pr][:, jj, :], inf_sb[q][:, j0 + jj, :], ident_b[:])

        def copy_x(pr, g, on_vector):
            if g == 0:
                grp[pr] = prep.tile([P, 2, 2 * P, 4], BF16, name="grp", tag="grp", align_bytes=64)
            dst = grp[pr][:].rearrange("p g c t -> p (g c t)").bitcast(F32)[:, g * H : (g + 1) * H]
            dst = dst.rearrange("p (jj r u) -> p jj r u", jj=2, u=2)
            src = xt[pr, g][:].rearrange("p jj u r -> p jj r u")
            if on_vector:
                nc.vector.tensor_copy(out=dst, in_=src)
            else:
                nc.scalar.copy(out=dst, in_=src)

        def copy_inf(pr):
            inf_t[pr] = prep.tile([P, 2 * P], BF16, name="inf_t", tag="inf_t", bufs=4)
            nc.scalar.copy(out=inf_t[pr][:], in_=it[pr][:].rearrange("p a b -> p (a b)"))

        def quantize(pr):
            codes[pr] = prep.tile([P, H], U32, name="codes", tag="codes", align_bytes=64)
            scales[pr] = prep.tile([P, H], U8, name="scales", tag="scales", align_bytes=64)
            nc.vector.quantize_mx(
                out=codes[pr][:].bitcast(FP8X4),
                scales=scales[pr][:],
                in_=grp[pr][:].rearrange("p g c t -> p (g c t)"),
            )

        def gate_matmuls(s):
            pr, jj = s // 2, s % 2
            for h in range(2):
                acc[s, h] = psum_acc.tile([P, H], F32, name="acc", tag="acc")
                for g in range(2):
                    cols = slice(g * 2 * P + jj * P, g * 2 * P + (jj + 1) * P)
                    nc.tensor.matmul_mx(
                        out=acc[s, h][:],
                        lhsT=codes[pr][:, cols].bitcast(FP8X4),
                        lhsT_scale=scales[pr][:, cols],
                        rhs=w_codes[g, h][:].bitcast(FP8X4),
                        rhs_scale=w_scales[g, h][:],
                        start=(g == 0),
                        stop=(g == 1),
                    )

        def shares_product(s):
            return s % 2 == 0 and s < NT - 2

        def flow_matmuls(s):
            pr, jj = s // 2, s % 2
            lhsT = inf_t[pr][:, jj * P : (jj + 1) * P]
            for h in range(2):
                width = H - GP if h == 1 and shares_product(s) else H
                fl[s, h] = psum_flow.tile([P, H], F32, name="fl", tag="fl")
                nc.tensor.matmul(
                    out=fl[s, h][:, 0:width],
                    lhsT=lhsT,
                    rhs=dec_sb[s // 8][:, h * H : h * H + width],
                    start=True,
                    stop=True,
                )
            if shares_product(s):
                fl_side[s] = psum_side.tile([P, GP], F32, name="fl_side", tag="fl_side")
                nc.tensor.matmul(out=fl_side[s][:], lhsT=lhsT, rhs=dec_sb[s // 8][:, D - GP : D], start=True, stop=True)

        def copy_flow(s):
            fl_sb[s] = ep.tile([P, GP], F32, name="fl_sb", tag="fl_sb")
            nc.scalar.copy(out=fl_sb[s][:], in_=fl_side[s][:])

        def product_on_gpsimd(s):
            nc.gpsimd.tensor_tensor(out=o0[s][:, D - GP : D], in0=fl_sb[s][:], in1=gate[s][:, D - GP : D], op=ALU.mult)

        def add_bias(s):
            pre[s] = ep.tile([P, D], F32, name="pre", tag="pre")
            for h in range(2):
                hs = slice(h * H, (h + 1) * H)
                nc.vector.tensor_tensor(out=pre[s][:, hs], in0=acc[s, h][:], in1=bias_sb[:, hs], op=ALU.add)

        def sigmoid(s):
            gate[s] = ep.tile([P, D], F32, name="gate", tag="gate")
            width = D if s < NT - 1 else H
            for c0 in range(0, D, width):
                nc.scalar.activation(out=gate[s][:, c0 : c0 + width], in_=pre[s][:, c0 : c0 + width], func=ACT.Sigmoid)

        def product(s, h):
            if h == 0:
                o0[s] = ep.tile([P, D], F32, name="o0", tag="o0", bufs=6)
            width = H - GP if h == 1 and shares_product(s) else H
            hs = slice(h * H, h * H + width)
            nc.vector.tensor_tensor(out=o0[s][:, hs], in0=fl[s, h][:, 0:width], in1=gate[s][:, hs], op=ALU.mult)

        def cast(s, c0, c1):
            q, j = s // 4, s % 4
            if j == 0 and c0 == 0:
                o1[q] = ep.tile([P, 4, D], FP8, name="o1", tag="o1")
            nc.scalar.activation(
                out=o1[q][:, j, c0:c1], in_=o0[s][:, c0:c1], func=ACT.Copy, scale=Y_SCALE, saturate=False
            )

        def shares_cast(s):
            return s % 2 == 1 and s < NT - 1

        def gpsimd_casts(s, pieces):
            for c0, c1 in pieces:
                nc.gpsimd.tensor_copy(out=o1[s // 4][:, s % 4, c0:c1], in_=scaled[s][:, c0:c1], saturate=False)

        def cast_on_gpsimd_first(s):
            scaled[s] = ep.tile([P, GC], F32, name="scaled", tag="scaled")
            for c0, c1 in ((0, H), (H, GC)):
                nc.gpsimd.tensor_scalar(
                    out=scaled[s][:, c0:c1], in0=o0[s][:, c0:c1], scalar1=Y_SCALE, scalar2=0.0, op0=ALU.mult, op1=ALU.add
                )
            gpsimd_casts(s, ((0, H),))

        def cast_on_gpsimd_rest(s):
            gpsimd_casts(s, ((H, GC),))

        def store_o0(s, c0, c1):
            nc.sync.dma_start(out=o0_v[s // 4, s % 4, :, c0:c1], in_=o0[s][:, c0:c1])

        def store_o1(q, j0, j1):
            nc.sync.dma_start(
                out=o1_v[q, :, j0 * D : j1 * D],
                in_=o1[q][:, j0:j1, :].rearrange("p j d -> p (j d)").bitcast(U8),
            )

        def finish(s):
            q, j = s // 4, s % 4
            if s < NT - 1:
                product(s, 0)
                product(s, 1)
                if shares_product(s):
                    product_on_gpsimd(s)
                store_o0(s, 0, D)
            else:
                for h in range(2):
                    product(s, h)
                    store_o0(s, h * H, (h + 1) * H)

        def finish_bytes(s):
            q, j = s // 4, s % 4
            if s < NT - 1:
                if shares_cast(s):
                    cast(s, GC, D)
                else:
                    cast(s, 0, D)
                if s == NT - 2:
                    store_o1(q, 0, 3)
            else:
                cast(s, 0, H)
                cast(s, H, D)
                store_o1(q, 3, 4)

        load_w(0)
        load_x(0, 0, 2)
        load_inf(0)
        load_w(1)
        nc.sync.dma_start(out=brow[0:1, :], in_=gate_b.rearrange("(o n) -> o n", o=1))
        load_x(0, 2, 4)
        load_x(1, 0, 4)
        load_inf(1)
        load_dec(0)
        keep_tensor_busy(8)
        w_interleave(0, 0)
        w_interleave(0, 1)
        transposes(0)
        w_quantize(0, 0)
        copy_x(0, 0, False)
        copy_x(0, 1, False)
        copy_inf(0)
        w_quantize(0, 1)
        quantize(0)
        w_interleave(1, 0)
        w_interleave(1, 1)
        w_quantize(1, 0)
        w_quantize(1, 1)
        bias_matmul()
        bias_copy()
        transposes(1)
        copy_x(1, 0, False)
        copy_x(1, 1, False)
        copy_inf(1)

        def pair_at(s, lead):
            if (s + lead) % 2 == 0 and 0 <= (s + lead) // 2 < NP:
                return (s + lead) // 2
            return None

        def on_vector(pr):
            return False

        for s in range(0, NT + 1):
            if s >= 0 and s % 4 == 0 and s // 4 + 2 < NQ:
                load_group(s // 4 + 2)
            pr_t, pr_x1, pr_q = pair_at(s, 4), pair_at(s, 3), pair_at(s, 2)
            if 0 <= s < NT:
                gate_matmuls(s)
            if pr_t is not None:
                transposes(pr_t)
            if 0 <= s - 1 < NT:
                flow_matmuls(s - 1)
                if shares_product(s - 1):
                    copy_flow(s - 1)
            if pr_t is not None:
                copy_x(pr_t, 0, False)
            if pr_x1 is not None:
                if not on_vector(pr_x1):
                    copy_x(pr_x1, 1, False)
                copy_inf(pr_x1)
            if 0 <= s < NT:
                add_bias(s)
            if pr_q is not None:
                quantize(pr_q)
            if 0 <= s < NT:
                sigmoid(s)
            if 0 <= s - 1 < NT:
                finish(s - 1)
                if shares_cast(s - 1):
                    cast_on_gpsimd_first(s - 1)
                if s - 2 >= 0 and shares_cast(s - 2):
                    cast_on_gpsimd_rest(s - 2)
                    if (s - 2) % 4 == 3:
                        store_o1((s - 2) // 4, 0, 4)
            if pr_x1 is not None and on_vector(pr_x1):
                copy_x(pr_x1, 1, True)
            if 0 <= s - 1 < NT:
                finish_bytes(s - 1)
